import numpy as np
import ml_dtypes


def mxq(x, axis, fmt="e4m3"):
    dtype, down = {"e4m3": (ml_dtypes.float8_e4m3fn, 7), "e5m2": (ml_dtypes.float8_e5m2, 14)}[fmt]
    v = np.moveaxis(np.asarray(x, np.float32).astype(ml_dtypes.bfloat16).astype(np.float64), axis, -1)
    blocks = v.reshape(v.shape[:-1] + (-1, 32))
    amax = np.abs(blocks).max(-1, keepdims=True)
    byte = np.maximum(np.where(amax > 0, np.frexp(amax)[1] - 1 + 127, 0) - down, 1)
    scale = np.exp2(byte - 127.0)
    codes = (blocks / scale).astype(np.float32).astype(dtype).astype(np.float64)
    return np.moveaxis((codes * scale).reshape(v.shape), -1, axis)


WIDE = False


def mx_kscale(k):
    if not WIDE:
        return np.ones(k)
    levels = np.array([10, -10, 5, -5, 0])
    a = np.random.permutation(np.resize(levels, k // 512 * 4)).reshape(k // 512, 4)
    idx = np.arange(k)
    return np.exp2(a[idx // 512, idx % 128 // 32])


BF16 = ml_dtypes.bfloat16


def bf(x):
    return np.asarray(x, np.float32).astype(BF16)


def f64(x):
    return np.asarray(x).astype(np.float64)


B, T, N, F_IN, F_OUT, K = 1, 8, 1024, 512, 128, 4


def delay(v, d):
    return np.concatenate([np.zeros((B, d, N, F_OUT)), v], axis=1)


def setup_inputs():
    s = mx_kscale(F_IN)
    return {"X": bf(np.random.standard_normal((B, T, N, F_IN)) * s),
            "S": bf(np.random.standard_normal((N, N)) / np.sqrt(N)),
            "w0": bf(np.random.standard_normal((F_OUT, F_IN)) / np.sqrt(F_IN) / s),
            "w1": bf(np.random.standard_normal((F_OUT, F_IN)) / np.sqrt(F_IN) / s)}


def reference(X, S, w0, w1):
    X = f64(X)
    z1 = mxq(f64(S), 1, "e4m3") @ mxq(X[:, :T - 1], 2, "e4m3")
    t0 = mxq(X, 3, "e4m3") @ mxq(f64(w0), 1, "e4m3").T
    t1 = mxq(z1, 3, "e4m3") @ mxq(f64(w1), 1, "e4m3").T
    return t0 + delay(t1, 1)

@@ -1,0 +1,219 @@
+from contextlib import ExitStack
+
+import concourse.mybir as mybir
+from concourse.masks import make_identity
+
+BF16 = mybir.dt.bfloat16
+F32 = mybir.dt.float32
+U32 = mybir.dt.uint32
+U8 = mybir.dt.uint8
+FP8X4 = mybir.dt.float8_e4m3fn_x4
+
+P = 128
+PACK = 4
+STEPS = 8
+NODES = 1024
+F_IN = 512
+F_OUT = 128
+HALVES = 2
+HALF = NODES // HALVES
+SLOTS = HALF // P
+F_CHUNKS = F_IN // P
+S_CHUNKS = 4
+S_ROWS = NODES // S_CHUNKS
+AHEAD = 2
+
+FLOPS = 2 * ((STEPS - 1) * NODES * NODES * F_IN + (2 * STEPS - 1) * NODES * F_IN * F_OUT)
+
+
+def block(i):
+    return slice(i * P, (i + 1) * P)
+
+
+def tile_stgnnlayer_pa_t_kernel(tc, X, S, w0, w1, out):
+    nc = tc.nc
+    with ExitStack() as ctx:
+        keep = ctx.enter_context(tc.tile_pool(name="keep", bufs=1))
+        grouped = ctx.enter_context(tc.tile_pool(name="grouped", bufs=2))
+        quantised = ctx.enter_context(tc.tile_pool(name="quantised", bufs=4))
+        results = ctx.enter_context(tc.tile_pool(name="results", bufs=3))
+        flipped = ctx.enter_context(tc.psum_pool(name="flipped", bufs=4))
+        sums = ctx.enter_context(tc.psum_pool(name="sums", bufs=4))
+        ctx.enter_context(tc.manual_schedule())
+
+        ident_f32 = keep.tile([P, P], F32, name="ident_f32")
+        make_identity(nc, ident_f32[:])
+        ident_bf16 = keep.tile([P, P], BF16, name="ident_bf16")
+        make_identity(nc, ident_bf16[:])
+
+        w0_sb = keep.tile([P, F_IN], BF16, name="w0_sb")
+        nc.scalar.dma_start(out=w0_sb[:], in_=w0)
+        w1_sb = keep.tile([P, F_IN], BF16, name="w1_sb")
+        nc.scalar.dma_start(out=w1_sb[:], in_=w1)
+
+        x_sb = {}
+
+        def load_x(t):
+            for h in range(HALVES):
+                x_half = keep.tile([P, SLOTS * F_IN], BF16, name="x_%d_%d" % (t, h))
+                nc.sync.dma_start(
+                    out=x_half[:].rearrange("p (u r) -> p u r", u=2),
+                    in_=X[0, t, h * HALF : (h + 1) * HALF, :].rearrange("(u p e) f -> p u (e f)", u=2, e=2),
+                )
+                x_sb[(t, h)] = x_half
+
+        s_sb = []
+        load_x(0)
+        for a in range(S_CHUNKS):
+            s_chunk = keep.tile([P, 2 * NODES], BF16, name="s_%d" % a)
+            nc.sync.dma_start(
+                out=s_chunk[:],
+                in_=S[a * S_ROWS : (a + 1) * S_ROWS, :].rearrange("(p e) m -> p (e m)", e=2),
+            )
+            s_sb.append(s_chunk)
+        for t in range(1, STEPS):
+            load_x(t)
+
+        def quantise(values, pool, label):
+            width = values.shape[1] // PACK
+            codes = pool.tile([P, width], U32, name=label + "_codes", tag=label + "_codes", align_bytes=64)
+            scales = pool.tile([P, width], U8, name=label + "_scales", tag=label + "_scales", align_bytes=64)
+            nc.vector.quantize_mx(out=codes[:].bitcast(FP8X4), scales=scales[:], in_=values)
+            return codes, scales
+
+        def mx_pass(acc, stationary, i, moving, k, start, stop):
+            nc.tensor.matmul_mx(
+                out=acc,
+                lhsT=stationary[0][:, block(i)].bitcast(FP8X4),
+                lhsT_scale=stationary[1][:, block(i)],
+                rhs=moving[0][:, block(k)].bitcast(FP8X4),
+                rhs_scale=moving[1][:, block(k)],
+                start=start,
+                stop=stop,
+            )
+
+        w0_ps = flipped.tile([P, 2, P], F32, name="w0_ps", tag="flipped")
+        for u in range(2):
+            nc.tensor.transpose(w0_ps[:, u, :], w0_sb[:].bitcast(F32)[:, block(u)], ident_f32[:])
+        w0_grouped = keep.tile([P, F_OUT * PACK], BF16, name="w0_grouped", align_bytes=64)
+        nc.scalar.copy(
+            out=w0_grouped[:].bitcast(F32).rearrange("p (o u) -> p o u", u=2),
+            in_=w0_ps[:].rearrange("p u o -> p o u"),
+        )
+        w1_ps = flipped.tile([P, F_CHUNKS, P], BF16, name="w1_ps", tag="flipped")
+        for c in range(F_CHUNKS):
+            nc.tensor.transpose(w1_ps[:, c, :], w1_sb[:, block(c)], ident_bf16[:])
+        w1_grouped = keep.tile([P, F_OUT * PACK], BF16, name="w1_grouped", align_bytes=64)
+        nc.scalar.copy(
+            out=w1_grouped[:].rearrange("p (o c) -> p o c", c=F_CHUNKS),
+            in_=w1_ps[:].rearrange("p c o -> p o c"),
+        )
+        w0_mx = quantise(w0_grouped[:], keep, "w0")
+        w1_mx = quantise(w1_grouped[:], keep, "w1")
+
+        xn_grouped = {}
+        xn_mx = {}
+        xt_grouped = {}
+        xt_mx = {}
+        st_mx = {}
+        z_grouped = {}
+        z_mx = {}
+
+        def regroup_x(t, g):
+            values = grouped.tile([P, F_IN * PACK], BF16, name="xn_grouped", tag="xn_grouped", align_bytes=64)
+            nc.vector.tensor_copy(
+                out=values[:].rearrange("p (c i j) -> p c j i", i=4, j=PACK),
+                in_=x_sb[(t, g)][:].rearrange("p (j c i) -> p c j i", j=PACK, i=4),
+            )
+            xn_grouped[(t, g)] = values
+
+        def transpose_x(t, h):
+            values = grouped.tile([P, HALF * PACK], BF16, name="xt_grouped", tag="xt_grouped", align_bytes=64)
+            pairs = values[:].bitcast(F32).rearrange("p (j n u) -> p j n u", j=SLOTS, u=2)
+            words = x_sb[(t, h)][:].bitcast(F32).rearrange("p (j w) -> p j w", j=SLOTS)
+            for b in range(SLOTS // 2):
+                xt_ps = flipped.tile([P, 2, 2, P], F32, name="xt_ps", tag="flipped")
+                for i in range(2):
+                    for u in range(2):
+                        nc.tensor.transpose(xt_ps[:, i, u, :], words[:, 2 * b + i, block(u)], ident_f32[:])
+                nc.scalar.copy(
+                    out=pairs[:, 2 * b : 2 * b + 2, :, :],
+                    in_=xt_ps[:].rearrange("p i u n -> p i n u"),
+                )
+            xt_grouped[(t, h)] = values
+
+        def prepare_s(a):
+            values = grouped.tile([P, 2 * HALVES * P * PACK], BF16, name="st_grouped", tag="st_grouped", align_bytes=64)
+            pairs = values[:].bitcast(F32).rearrange("p (e g n u) -> p e g n u", e=2, g=HALVES, u=2)
+            words = s_sb[a][:].bitcast(F32).rearrange("p (e w) -> p e w", e=2)
+            for e in range(2):
+                st_ps = sums.tile([P, 2 * HALVES, P], F32, name="st_ps", tag="sums")
+                for k in range(2 * HALVES):
+                    nc.tensor.transpose(st_ps[:, k, :], words[:, e, block(k)], ident_f32[:])
+                nc.scalar.copy(
+                    out=pairs[:, e, :, :, :],
+                    in_=st_ps[:].rearrange("p (g u) n -> p g n u", u=2),
+                )
+            st_mx[a] = quantise(values[:], keep, "st_%d" % a)
+
+        def shift(t, h, j):
+            if j == 0:
+                z_half = grouped.tile([P, HALF * PACK], BF16, name="z_grouped", tag="z_grouped", align_bytes=64)
+                z_grouped[(t, h)] = z_half
+            a, e = divmod(SLOTS * h + j, 2)
+            z_ps = sums.tile([P, F_CHUNKS, P], F32, name="z_ps", tag="sums")
+            for c in range(F_CHUNKS):
+                for g in range(HALVES):
+                    mx_pass(z_ps[:, c, :], xn_mx[(t, g)], c, st_mx[a], HALVES * e + g, g == 0, g == HALVES - 1)
+            nc.scalar.copy(
+                out=z_grouped[(t, h)][:].rearrange("p (j n c) -> p j n c", j=SLOTS, c=F_CHUNKS)[:, j, :, :],
+                in_=z_ps[:].rearrange("p c n -> p n c"),
+            )
+
+        def taps(t, h):
+            y_ps = sums.tile([P, SLOTS, F_OUT], F32, name="y_ps", tag="sums")
+            for j in range(SLOTS):
+                mx_pass(y_ps[:, j, :], xt_mx[(t, h)], j, w0_mx, 0, True, t == 0)
+                if t > 0:
+                    mx_pass(y_ps[:, j, :], z_mx[(t - 1, h)], j, w1_mx, 0, False, True)
+            y_sb = results.tile([P, SLOTS * F_OUT], F32, name="y_sb", tag="y_sb")
+            nc.vector.tensor_copy(out=y_sb[:], in_=y_ps[:].rearrange("p j o -> p (j o)"))
+            nc.sync.dma_start(
+                out=out[0, t, h * HALF : (h + 1) * HALF, :].rearrange("(u p e) o -> p u (e o)", u=2, e=2),
+                in_=y_sb[:].rearrange("p (u r) -> p u r", u=2),
+            )
+
+        for g in range(HALVES):
+            regroup_x(0, g)
+        for g in range(HALVES):
+            xn_mx[(0, g)] = quantise(xn_grouped[(0, g)][:], quantised, "xn")
+        for h in range(HALVES):
+            transpose_x(0, h)
+        for a in range(AHEAD):
+            prepare_s(a)
+        for h in range(HALVES):
+            xt_mx[(0, h)] = quantise(xt_grouped[(0, h)][:], quantised, "xt")
+
+        for t in range(STEPS - 1):
+            for h in range(HALVES):
+                for j in range(SLOTS):
+                    shift(t, h, j)
+                    a, e = divmod(SLOTS * h + j, 2)
+                    if t == 0 and e == 1 and a + AHEAD < S_CHUNKS:
+                        prepare_s(a + AHEAD)
+                if h == 0 and t + 1 < STEPS - 1:
+                    for g in range(HALVES):
+                        regroup_x(t + 1, g)
+                taps(t, h)
+                z_mx[(t, h)] = quantise(z_grouped[(t, h)][:], quantised, "z")
+                if h == 0:
+                    if t + 1 < STEPS - 1:
+                        for g in range(HALVES):
+                            xn_mx[(t + 1, g)] = quantise(xn_grouped[(t + 1, g)][:], quantised, "xn")
+                    for k in range(HALVES):
+                        transpose_x(t + 1, k)
+                    for k in range(HALVES):
+                        xt_mx[(t + 1, k)] = quantise(xt_grouped[(t + 1, k)][:], quantised, "xt")
+
+        for h in range(HALVES):
+            taps(STEPS - 1, h)

@@ -19,9 +19,7 @@ HALVES = 2
 HALF = NODES // HALVES
 SLOTS = HALF // P
 F_CHUNKS = F_IN // P
-S_CHUNKS = 4
-S_ROWS = NODES // S_CHUNKS
-AHEAD = 2
+S_ROWS = 2 * P
 
 FLOPS = 2 * ((STEPS - 1) * NODES * NODES * F_IN + (2 * STEPS - 1) * NODES * F_IN * F_OUT)
 
@@ -36,7 +34,7 @@ def tile_stgnnlayer_pa_t_kernel(tc, X, S, w0, w1, out):
         keep = ctx.enter_context(tc.tile_pool(name="keep", bufs=1))
         grouped = ctx.enter_context(tc.tile_pool(name="grouped", bufs=2))
         quantised = ctx.enter_context(tc.tile_pool(name="quantised", bufs=4))
-        results = ctx.enter_context(tc.tile_pool(name="results", bufs=3))
+        results = ctx.enter_context(tc.tile_pool(name="results", bufs=4))
         flipped = ctx.enter_context(tc.psum_pool(name="flipped", bufs=4))
         sums = ctx.enter_context(tc.psum_pool(name="sums", bufs=4))
         ctx.enter_context(tc.manual_schedule())
@@ -64,7 +62,7 @@ def tile_stgnnlayer_pa_t_kernel(tc, X, S, w0, w1, out):
 
         s_sb = []
         load_x(0)
-        for a in range(S_CHUNKS):
+        for a in range(NODES // S_ROWS):
             s_chunk = keep.tile([P, 2 * NODES], BF16, name="s_%d" % a)
             nc.sync.dma_start(
                 out=s_chunk[:],
@@ -136,35 +134,35 @@ def tile_stgnnlayer_pa_t_kernel(tc, X, S, w0, w1, out):
                 for i in range(2):
                     for u in range(2):
                         nc.tensor.transpose(xt_ps[:, i, u, :], words[:, 2 * b + i, block(u)], ident_f32[:])
-                nc.scalar.copy(
-                    out=pairs[:, 2 * b : 2 * b + 2, :, :],
-                    in_=xt_ps[:].rearrange("p i u n -> p i n u"),
-                )
+                if t < STEPS - 1:
+                    nc.scalar.copy(out=pairs[:, 2 * b : 2 * b + 2, :, :], in_=xt_ps[:].rearrange("p i u n -> p i n u"))
+                else:
+                    nc.vector.tensor_copy(
+                        out=pairs[:, 2 * b : 2 * b + 2, :, :], in_=xt_ps[:].rearrange("p i u n -> p i n u")
+                    )
             xt_grouped[(t, h)] = values
 
-        def prepare_s(a):
-            values = grouped.tile([P, 2 * HALVES * P * PACK], BF16, name="st_grouped", tag="st_grouped", align_bytes=64)
-            pairs = values[:].bitcast(F32).rearrange("p (e g n u) -> p e g n u", e=2, g=HALVES, u=2)
+        def prepare_s(s):
+            a, e = divmod(s, 2)
+            values = grouped.tile([P, HALVES * P * PACK], BF16, name="st_grouped", tag="st_grouped", align_bytes=64)
             words = s_sb[a][:].bitcast(F32).rearrange("p (e w) -> p e w", e=2)
-            for e in range(2):
-                st_ps = sums.tile([P, 2 * HALVES, P], F32, name="st_ps", tag="sums")
-                for k in range(2 * HALVES):
-                    nc.tensor.transpose(st_ps[:, k, :], words[:, e, block(k)], ident_f32[:])
-                nc.scalar.copy(
-                    out=pairs[:, e, :, :, :],
-                    in_=st_ps[:].rearrange("p (g u) n -> p g n u", u=2),
-                )
-            st_mx[a] = quantise(values[:], keep, "st_%d" % a)
+            st_ps = sums.tile([P, 2 * HALVES, P], F32, name="st_ps", tag="sums")
+            for k in range(2 * HALVES):
+                nc.tensor.transpose(st_ps[:, k, :], words[:, e, block(k)], ident_f32[:])
+            nc.scalar.copy(
+                out=values[:].bitcast(F32).rearrange("p (g n u) -> p g n u", g=HALVES, u=2),
+                in_=st_ps[:].rearrange("p (g u) n -> p g n u", u=2),
+            )
+            st_mx[s] = quantise(values[:], keep, "st_%d" % s)
 
         def shift(t, h, j):
             if j == 0:
                 z_half = grouped.tile([P, HALF * PACK], BF16, name="z_grouped", tag="z_grouped", align_bytes=64)
                 z_grouped[(t, h)] = z_half
-            a, e = divmod(SLOTS * h + j, 2)
             z_ps = sums.tile([P, F_CHUNKS, P], F32, name="z_ps", tag="sums")
             for c in range(F_CHUNKS):
                 for g in range(HALVES):
-                    mx_pass(z_ps[:, c, :], xn_mx[(t, g)], c, st_mx[a], HALVES * e + g, g == 0, g == HALVES - 1)
+                    mx_pass(z_ps[:, c, :], xn_mx[(t, g)], c, st_mx[SLOTS * h + j], g, g == 0, g == HALVES - 1)
             nc.scalar.copy(
                 out=z_grouped[(t, h)][:].rearrange("p (j n c) -> p j n c", j=SLOTS, c=F_CHUNKS)[:, j, :, :],
                 in_=z_ps[:].rearrange("p c n -> p n c"),
@@ -189,31 +187,38 @@ def tile_stgnnlayer_pa_t_kernel(tc, X, S, w0, w1, out):
             xn_mx[(0, g)] = quantise(xn_grouped[(0, g)][:], quantised, "xn")
         for h in range(HALVES):
             transpose_x(0, h)
-        for a in range(AHEAD):
-            prepare_s(a)
+        for s in range(SLOTS):
+            prepare_s(s)
         for h in range(HALVES):
             xt_mx[(0, h)] = quantise(xt_grouped[(0, h)][:], quantised, "xt")
 
         for t in range(STEPS - 1):
-            for h in range(HALVES):
-                for j in range(SLOTS):
-                    shift(t, h, j)
-                    a, e = divmod(SLOTS * h + j, 2)
-                    if t == 0 and e == 1 and a + AHEAD < S_CHUNKS:
-                        prepare_s(a + AHEAD)
-                if h == 0 and t + 1 < STEPS - 1:
+            shifted_next = t + 1 < STEPS - 1
+            for j in range(SLOTS):
+                shift(t, 0, j)
+                if t == 0 and j % 2 == 0:
+                    prepare_s(SLOTS + j)
+                    prepare_s(SLOTS + j + 1)
+                if j == 0 and shifted_next:
                     for g in range(HALVES):
                         regroup_x(t + 1, g)
-                taps(t, h)
-                z_mx[(t, h)] = quantise(z_grouped[(t, h)][:], quantised, "z")
-                if h == 0:
-                    if t + 1 < STEPS - 1:
-                        for g in range(HALVES):
-                            xn_mx[(t + 1, g)] = quantise(xn_grouped[(t + 1, g)][:], quantised, "xn")
-                    for k in range(HALVES):
-                        transpose_x(t + 1, k)
-                    for k in range(HALVES):
-                        xt_mx[(t + 1, k)] = quantise(xt_grouped[(t + 1, k)][:], quantised, "xt")
+            if shifted_next:
+                for g in range(HALVES):
+                    xn_mx[(t + 1, g)] = quantise(xn_grouped[(t + 1, g)][:], quantised, "xn")
+            taps(t, 0)
+            z_mx[(t, 0)] = quantise(z_grouped[(t, 0)][:], quantised, "z")
+            for h in range(HALVES):
+                transpose_x(t + 1, h)
+            for h in range(HALVES):
+                xt_mx[(t + 1, h)] = quantise(xt_grouped[(t + 1, h)][:], quantised, "xt")
+            for j in range(SLOTS):
+                shift(t, 1, j)
+            if shifted_next:
+                taps(t, 1)
+                z_mx[(t, 1)] = quantise(z_grouped[(t, 1)][:], quantised, "z")
+            else:
+                z_mx[(t, 1)] = quantise(z_grouped[(t, 1)][:], quantised, "z")
+                taps(t, 1)
 
         for h in range(HALVES):
             taps(STEPS - 1, h)

@@ -207,12 +207,13 @@ def tile_stgnnlayer_pa_t_kernel(tc, X, S, w0, w1, out):
                     xn_mx[(t + 1, g)] = quantise(xn_grouped[(t + 1, g)][:], quantised, "xn")
             taps(t, 0)
             z_mx[(t, 0)] = quantise(z_grouped[(t, 0)][:], quantised, "z")
-            for h in range(HALVES):
-                transpose_x(t + 1, h)
-            for h in range(HALVES):
-                xt_mx[(t + 1, h)] = quantise(xt_grouped[(t + 1, h)][:], quantised, "xt")
+            transpose_x(t + 1, 0)
             for j in range(SLOTS):
                 shift(t, 1, j)
+                if j == 1:
+                    transpose_x(t + 1, 1)
+                    for h in range(HALVES):
+                        xt_mx[(t + 1, h)] = quantise(xt_grouped[(t + 1, h)][:], quantised, "xt")
             if shifted_next:
                 taps(t, 1)
                 z_mx[(t, 1)] = quantise(z_grouped[(t, 1)][:], quantised, "z")

@@ -34,43 +34,56 @@ def tile_stgnnlayer_pa_t_kernel(tc, X, S, w0, w1, out):
         keep = ctx.enter_context(tc.tile_pool(name="keep", bufs=1))
         grouped = ctx.enter_context(tc.tile_pool(name="grouped", bufs=2))
         quantised = ctx.enter_context(tc.tile_pool(name="quantised", bufs=4))
-        results = ctx.enter_context(tc.tile_pool(name="results", bufs=4))
+        results = ctx.enter_context(tc.tile_pool(name="results", bufs=8))
         flipped = ctx.enter_context(tc.psum_pool(name="flipped", bufs=4))
         sums = ctx.enter_context(tc.psum_pool(name="sums", bufs=4))
         ctx.enter_context(tc.manual_schedule())
 
+        zeros = keep.tile([P, 512], BF16, name="zeros")
+        nc.vector.memset(zeros[:], 0.0)
         ident_f32 = keep.tile([P, P], F32, name="ident_f32")
         make_identity(nc, ident_f32[:])
         ident_bf16 = keep.tile([P, P], BF16, name="ident_bf16")
         make_identity(nc, ident_bf16[:])
 
-        w0_sb = keep.tile([P, F_IN], BF16, name="w0_sb")
-        nc.scalar.dma_start(out=w0_sb[:], in_=w0)
-        w1_sb = keep.tile([P, F_IN], BF16, name="w1_sb")
-        nc.scalar.dma_start(out=w1_sb[:], in_=w1)
-
         x_sb = {}
+        s_sb = {}
+        w_sb = {}
 
-        def load_x(t):
-            for h in range(HALVES):
-                x_half = keep.tile([P, SLOTS * F_IN], BF16, name="x_%d_%d" % (t, h))
-                nc.sync.dma_start(
-                    out=x_half[:].rearrange("p (u r) -> p u r", u=2),
-                    in_=X[0, t, h * HALF : (h + 1) * HALF, :].rearrange("(u p e) f -> p u (e f)", u=2, e=2),
-                )
-                x_sb[(t, h)] = x_half
-
-        s_sb = []
-        load_x(0)
-        for a in range(NODES // S_ROWS):
-            s_chunk = keep.tile([P, 2 * NODES], BF16, name="s_%d" % a)
+        def load_x(t, h):
+            x_half = keep.tile([P, SLOTS * F_IN], BF16, name="x_%d_%d" % (t, h))
             nc.sync.dma_start(
-                out=s_chunk[:],
-                in_=S[a * S_ROWS : (a + 1) * S_ROWS, :].rearrange("(p e) m -> p (e m)", e=2),
+                out=x_half[:].rearrange("p (u r) -> p u r", u=2),
+                in_=X[0, t, h * HALF : (h + 1) * HALF, :].rearrange("(u p e) f -> p u (e f)", u=2, e=2),
             )
-            s_sb.append(s_chunk)
+            x_sb[(t, h)] = x_half
+
+        def load_s(s):
+            a, e = divmod(s, 2)
+            s_slot = keep.tile([P, NODES], BF16, name="s_%d" % s)
+            nc.sync.dma_start(
+                out=s_slot[:],
+                in_=S[a * S_ROWS : (a + 1) * S_ROWS, :].rearrange("(p e) m -> p e m", e=2)[:, e, :],
+            )
+            s_sb[s] = s_slot
+
+        def load_w(tap):
+            w_tap = keep.tile([P, F_IN], BF16, name="w%d_sb" % tap)
+            nc.sync.dma_start(out=w_tap[:], in_=(w0, w1)[tap])
+            w_sb[tap] = w_tap
+
+        load_x(0, 0)
+        load_s(0)
+        load_x(0, 1)
+        for s in range(1, SLOTS):
+            load_s(s)
+        for s in range(SLOTS, 2 * SLOTS):
+            load_s(s)
+        for tap in range(2):
+            load_w(tap)
         for t in range(1, STEPS):
-            load_x(t)
+            for h in range(HALVES):
+                load_x(t, h)
 
         def quantise(values, pool, label):
             width = values.shape[1] // PACK
@@ -90,72 +103,102 @@ def tile_stgnnlayer_pa_t_kernel(tc, X, S, w0, w1, out):
                 stop=stop,
             )
 
-        w0_ps = flipped.tile([P, 2, P], F32, name="w0_ps", tag="flipped")
-        for u in range(2):
-            nc.tensor.transpose(w0_ps[:, u, :], w0_sb[:].bitcast(F32)[:, block(u)], ident_f32[:])
-        w0_grouped = keep.tile([P, F_OUT * PACK], BF16, name="w0_grouped", align_bytes=64)
-        nc.scalar.copy(
-            out=w0_grouped[:].bitcast(F32).rearrange("p (o u) -> p o u", u=2),
-            in_=w0_ps[:].rearrange("p u o -> p o u"),
-        )
-        w1_ps = flipped.tile([P, F_CHUNKS, P], BF16, name="w1_ps", tag="flipped")
-        for c in range(F_CHUNKS):
-            nc.tensor.transpose(w1_ps[:, c, :], w1_sb[:, block(c)], ident_bf16[:])
-        w1_grouped = keep.tile([P, F_OUT * PACK], BF16, name="w1_grouped", align_bytes=64)
-        nc.scalar.copy(
-            out=w1_grouped[:].rearrange("p (o c) -> p o c", c=F_CHUNKS),
-            in_=w1_ps[:].rearrange("p c o -> p o c"),
-        )
-        w0_mx = quantise(w0_grouped[:], keep, "w0")
-        w1_mx = quantise(w1_grouped[:], keep, "w1")
+        def copy_on(engine, out, in_):
+            if engine:
+                nc.scalar.copy(out=out, in_=in_)
+            else:
+                nc.vector.tensor_copy(out=out, in_=in_)
+
+        def warm(n):
+            warm_ps = sums.tile([P, 512], F32, name="warm_ps", tag="sums")
+            for k in range(n):
+                nc.tensor.matmul(warm_ps[:], lhsT=zeros[:, :P], rhs=zeros[:], start=True, stop=True)
+
+        w_grouped = {}
+        w_mx = {}
+
+        def flip_weights():
+            w0_ps = flipped.tile([P, 2, P], F32, name="w0_ps", tag="flipped")
+            for u in range(2):
+                nc.tensor.transpose(w0_ps[:, u, :], w_sb[0][:].bitcast(F32)[:, block(u)], ident_f32[:])
+            w0_grouped = keep.tile([P, F_OUT * PACK], BF16, name="w0_grouped", align_bytes=64)
+            nc.scalar.copy(
+                out=w0_grouped[:].bitcast(F32).rearrange("p (o u) -> p o u", u=2),
+                in_=w0_ps[:].rearrange("p u o -> p o u"),
+            )
+            w1_ps = flipped.tile([P, F_CHUNKS, P], BF16, name="w1_ps", tag="flipped")
+            for c in range(F_CHUNKS):
+                nc.tensor.transpose(w1_ps[:, c, :], w_sb[1][:, block(c)], ident_bf16[:])
+            w1_grouped = keep.tile([P, F_OUT * PACK], BF16, name="w1_grouped", align_bytes=64)
+            nc.scalar.copy(
+                out=w1_grouped[:].rearrange("p (o c) -> p o c", c=F_CHUNKS),
+                in_=w1_ps[:].rearrange("p c o -> p o c"),
+            )
+            w_grouped[0] = w0_grouped
+            w_grouped[1] = w1_grouped
+
+        def quantise_weights():
+            for tap in range(2):
+                w_mx[tap] = quantise(w_grouped[tap][:], keep, "w%d" % tap)
 
         xn_grouped = {}
         xn_mx = {}
         xt_grouped = {}
         xt_mx = {}
+        st_grouped = {}
         st_mx = {}
         z_grouped = {}
         z_mx = {}
 
-        def regroup_x(t, g):
+        def regroup_x(t, g, scalar_from=F_IN):
             values = grouped.tile([P, F_IN * PACK], BF16, name="xn_grouped", tag="xn_grouped", align_bytes=64)
-            nc.vector.tensor_copy(
-                out=values[:].rearrange("p (c i j) -> p c j i", i=4, j=PACK),
-                in_=x_sb[(t, g)][:].rearrange("p (j c i) -> p c j i", j=PACK, i=4),
-            )
+            for lo, hi, engine in ((0, scalar_from, False), (scalar_from, F_IN, True)):
+                if lo < hi:
+                    copy_on(
+                        engine,
+                        values[:, lo * PACK : hi * PACK].rearrange("p (c i j) -> p c j i", i=4, j=PACK),
+                        x_sb[(t, g)][:].rearrange("p (j f) -> p j f", j=PACK)[:, :, lo:hi].rearrange("p j (c i) -> p c j i", i=4),
+                    )
             xn_grouped[(t, g)] = values
 
-        def transpose_x(t, h):
-            values = grouped.tile([P, HALF * PACK], BF16, name="xt_grouped", tag="xt_grouped", align_bytes=64)
-            pairs = values[:].bitcast(F32).rearrange("p (j n u) -> p j n u", j=SLOTS, u=2)
-            words = x_sb[(t, h)][:].bitcast(F32).rearrange("p (j w) -> p j w", j=SLOTS)
-            for b in range(SLOTS // 2):
-                xt_ps = flipped.tile([P, 2, 2, P], F32, name="xt_ps", tag="flipped")
-                for i in range(2):
-                    for u in range(2):
-                        nc.tensor.transpose(xt_ps[:, i, u, :], words[:, 2 * b + i, block(u)], ident_f32[:])
-                if t < STEPS - 1:
-                    nc.scalar.copy(out=pairs[:, 2 * b : 2 * b + 2, :, :], in_=xt_ps[:].rearrange("p i u n -> p i n u"))
-                else:
-                    nc.vector.tensor_copy(
-                        out=pairs[:, 2 * b : 2 * b + 2, :, :], in_=xt_ps[:].rearrange("p i u n -> p i n u")
-                    )
-            xt_grouped[(t, h)] = values
+        def quantise_xn(t, g):
+            xn_mx[(t, g)] = quantise(xn_grouped[(t, g)][:], quantised, "xn")
 
-        def prepare_s(s):
-            a, e = divmod(s, 2)
-            values = grouped.tile([P, HALVES * P * PACK], BF16, name="st_grouped", tag="st_grouped", align_bytes=64)
-            words = s_sb[a][:].bitcast(F32).rearrange("p (e w) -> p e w", e=2)
+        def flip_x(t, h, b, engine):
+            if b == 0:
+                if t == 0:
+                    values = keep.tile([P, HALF * PACK], BF16, name="xt_grouped_0_%d" % h, align_bytes=64)
+                else:
+                    values = grouped.tile([P, HALF * PACK], BF16, name="xt_grouped", tag="xt_grouped", bufs=3, align_bytes=64)
+                xt_grouped[(t, h)] = values
+            pairs = xt_grouped[(t, h)][:].bitcast(F32).rearrange("p (j n u) -> p j n u", j=SLOTS, u=2)
+            words = x_sb[(t, h)][:].bitcast(F32).rearrange("p (j w) -> p j w", j=SLOTS)
+            xt_ps = flipped.tile([P, 2, 2, P], F32, name="xt_ps", tag="flipped")
+            for i in range(2):
+                for u in range(2):
+                    nc.tensor.transpose(xt_ps[:, i, u, :], words[:, 2 * b + i, block(u)], ident_f32[:])
+            copy_on(engine, pairs[:, 2 * b : 2 * b + 2, :, :], xt_ps[:].rearrange("p i u n -> p i n u"))
+
+        def quantise_xt(t, h):
+            xt_mx[(t, h)] = quantise(xt_grouped[(t, h)][:], quantised, "xt")
+
+        def flip_s(s, engine):
+            values = grouped.tile([P, HALVES * P * PACK], BF16, name="st_grouped", tag="st_grouped", bufs=4, align_bytes=64)
+            words = s_sb[s][:].bitcast(F32)
             st_ps = sums.tile([P, 2 * HALVES, P], F32, name="st_ps", tag="sums")
             for k in range(2 * HALVES):
-                nc.tensor.transpose(st_ps[:, k, :], words[:, e, block(k)], ident_f32[:])
-            nc.scalar.copy(
-                out=values[:].bitcast(F32).rearrange("p (g n u) -> p g n u", g=HALVES, u=2),
-                in_=st_ps[:].rearrange("p (g u) n -> p g n u", u=2),
+                nc.tensor.transpose(st_ps[:, k, :], words[:, block(k)], ident_f32[:])
+            copy_on(
+                engine,
+                values[:].bitcast(F32).rearrange("p (g n u) -> p g n u", g=HALVES, u=2),
+                st_ps[:].rearrange("p (g u) n -> p g n u", u=2),
             )
-            st_mx[s] = quantise(values[:], keep, "st_%d" % s)
+            st_grouped[s] = values
 
-        def shift(t, h, j):
+        def quantise_s(s):
+            st_mx[s] = quantise(st_grouped[s][:], keep, "st_%d" % s)
+
+        def shift(t, h, j, engine=True):
             if j == 0:
                 z_half = grouped.tile([P, HALF * PACK], BF16, name="z_grouped", tag="z_grouped", align_bytes=64)
                 z_grouped[(t, h)] = z_half
@@ -163,63 +206,121 @@ def tile_stgnnlayer_pa_t_kernel(tc, X, S, w0, w1, out):
             for c in range(F_CHUNKS):
                 for g in range(HALVES):
                     mx_pass(z_ps[:, c, :], xn_mx[(t, g)], c, st_mx[SLOTS * h + j], g, g == 0, g == HALVES - 1)
-            nc.scalar.copy(
-                out=z_grouped[(t, h)][:].rearrange("p (j n c) -> p j n c", j=SLOTS, c=F_CHUNKS)[:, j, :, :],
-                in_=z_ps[:].rearrange("p c n -> p n c"),
+            copy_on(
+                engine,
+                z_grouped[(t, h)][:].rearrange("p (j n c) -> p j n c", j=SLOTS, c=F_CHUNKS)[:, j, :, :],
+                z_ps[:].rearrange("p c n -> p n c"),
             )
 
-        def taps(t, h):
-            y_ps = sums.tile([P, SLOTS, F_OUT], F32, name="y_ps", tag="sums")
-            for j in range(SLOTS):
-                mx_pass(y_ps[:, j, :], xt_mx[(t, h)], j, w0_mx, 0, True, t == 0)
+        def quantise_z(t, h, first=0, slots=SLOTS):
+            values = z_grouped[(t, h)][:, first * P * PACK : (first + slots) * P * PACK]
+            operand = quantise(values, quantised, "z" if slots == SLOTS else "z_part")
+            for j in range(slots):
+                z_mx[(t, h, first + j)] = (operand, j)
+
+        def taps(t, h, engine=False, first=0, slots=SLOTS):
+            y_ps = sums.tile([P, slots, F_OUT], F32, name="y_ps", tag="sums")
+            for j in range(slots):
+                mx_pass(y_ps[:, j, :], xt_mx[(t, h)], first + j, w_mx[0], 0, True, t == 0)
                 if t > 0:
-                    mx_pass(y_ps[:, j, :], z_mx[(t - 1, h)], j, w1_mx, 0, False, True)
-            y_sb = results.tile([P, SLOTS * F_OUT], F32, name="y_sb", tag="y_sb")
-            nc.vector.tensor_copy(out=y_sb[:], in_=y_ps[:].rearrange("p j o -> p (j o)"))
+                    operand, i = z_mx[(t - 1, h, first + j)]
+                    mx_pass(y_ps[:, j, :], operand, i, w_mx[1], 0, False, True)
+            y_sb = results.tile([P, slots * F_OUT], F32, name="y_sb", tag="y_sb")
+            copy_on(engine, y_sb[:], y_ps[:].rearrange("p j o -> p (j o)"))
             nc.sync.dma_start(
-                out=out[0, t, h * HALF : (h + 1) * HALF, :].rearrange("(u p e) o -> p u (e o)", u=2, e=2),
-                in_=y_sb[:].rearrange("p (u r) -> p u r", u=2),
+                out=out[0, t, h * HALF : (h + 1) * HALF, :].rearrange("(u p e) o -> p u (e o)", u=2, e=2)[:, first // 2 : (first + slots) // 2, :],
+                in_=y_sb[:].rearrange("p (u r) -> p u r", r=2 * F_OUT),
             )
 
-        for g in range(HALVES):
-            regroup_x(0, g)
-        for g in range(HALVES):
-            xn_mx[(0, g)] = quantise(xn_grouped[(0, g)][:], quantised, "xn")
-        for h in range(HALVES):
-            transpose_x(0, h)
-        for s in range(SLOTS):
-            prepare_s(s)
-        for h in range(HALVES):
-            xt_mx[(0, h)] = quantise(xt_grouped[(0, h)][:], quantised, "xt")
+        warm(12)
+        regroup_x(0, 0, 384)
+        flip_x(0, 0, 0, True)
+        flip_x(0, 0, 1, True)
+        flip_s(0, True)
+        warm(4)
+        quantise_xn(0, 0)
+        regroup_x(0, 1, 384)
+        flip_s(1, True)
+        flip_s(2, True)
+        warm(1)
+        quantise_s(0)
+        quantise_xn(0, 1)
+        quantise_s(1)
+        flip_s(3, False)
+        quantise_s(2)
+        quantise_s(3)
 
-        for t in range(STEPS - 1):
-            shifted_next = t + 1 < STEPS - 1
-            for j in range(SLOTS):
-                shift(t, 0, j)
-                if t == 0 and j % 2 == 0:
-                    prepare_s(SLOTS + j)
-                    prepare_s(SLOTS + j + 1)
-                if j == 0 and shifted_next:
-                    for g in range(HALVES):
-                        regroup_x(t + 1, g)
-            if shifted_next:
-                for g in range(HALVES):
-                    xn_mx[(t + 1, g)] = quantise(xn_grouped[(t + 1, g)][:], quantised, "xn")
-            taps(t, 0)
-            z_mx[(t, 0)] = quantise(z_grouped[(t, 0)][:], quantised, "z")
-            transpose_x(t + 1, 0)
-            for j in range(SLOTS):
-                shift(t, 1, j)
-                if j == 1:
-                    transpose_x(t + 1, 1)
-                    for h in range(HALVES):
-                        xt_mx[(t + 1, h)] = quantise(xt_grouped[(t + 1, h)][:], quantised, "xt")
-            if shifted_next:
-                taps(t, 1)
-                z_mx[(t, 1)] = quantise(z_grouped[(t, 1)][:], quantised, "z")
-            else:
-                z_mx[(t, 1)] = quantise(z_grouped[(t, 1)][:], quantised, "z")
-                taps(t, 1)
+        shift(0, 0, 0)
+        shift(0, 0, 1)
+        flip_s(4, False)
+        flip_s(5, False)
+        quantise_s(4)
+        quantise_s(5)
+        shift(0, 0, 2)
+        shift(0, 0, 3)
+        flip_s(6, False)
+        flip_x(0, 1, 0, True)
+        flip_x(0, 1, 1, True)
+        regroup_x(1, 0)
+        quantise_s(6)
+        shift(0, 1, 0)
+        shift(0, 1, 1)
+        flip_s(7, True)
+        flip_x(1, 0, 0, True)
+        flip_x(1, 0, 1, True)
+        regroup_x(1, 1)
+        quantise_s(7)
+        shift(0, 1, 2)
+        shift(0, 1, 3)
+        for g in range(2):
+            quantise_xn(1, g)
+        quantise_z(0, 0)
+        flip_weights()
+        for b in range(2):
+            flip_x(1, 1, b, True)
+        quantise_xt(1, 0)
+        quantise_weights()
+        quantise_z(0, 1)
 
-        for h in range(HALVES):
-            taps(STEPS - 1, h)
+        banks = [(x, h, b) for x in range(2, STEPS) for h in range(HALVES) for b in range(2)]
+        done = []
+        quantise_xt(1, 1)
+        for n in range(SLOTS * HALVES, SLOTS * HALVES * (STEPS - 1)):
+            t, slot = divmod(n, SLOTS * HALVES)
+            h, j = divmod(slot, SLOTS)
+            more = t + 1 < STEPS - 1
+            shift(t, h, j)
+            if slot == 0 and more:
+                regroup_x(t + 1, 0)
+            if slot == 3:
+                if more:
+                    quantise_xn(t + 1, 0)
+                    quantise_xn(t + 1, 1)
+                taps(t, 0)
+                quantise_z(t, 0)
+            if slot == 7 and more:
+                taps(t, 1)
+                quantise_z(t, 1)
+            if n % 6 == 3 and banks:
+                for k in range(3):
+                    x, xh, b = banks.pop(0)
+                    flip_x(x, xh, b, True)
+                    if b == 1:
+                        done.append((x, xh))
+            if n % 6 == 5 and n > 12:
+                for x, xh in done:
+                    quantise_xt(x, xh)
+                done = []
+            if slot == 1 and more:
+                regroup_x(t + 1, 1)
+            if t == STEPS - 2 and slot in (1, 2):
+                quantise_xt(0, slot - 1)
+            if t == STEPS - 2 and slot in (4, 5):
+                taps(0, slot - 4)
+        t = STEPS - 2
+        quantise_z(t, 1, 0, 2)
+        taps(t, 1)
+        quantise_z(t, 1, 2, 2)
+        taps(t + 1, 0, True)
+        taps(t + 1, 1, True, 0, 2)
+        taps(t + 1, 1, False, 2, 2)

@@ -35,8 +35,8 @@ def tile_stgnnlayer_pa_t_kernel(tc, X, S, w0, w1, out):
         grouped = ctx.enter_context(tc.tile_pool(name="grouped", bufs=2))
         quantised = ctx.enter_context(tc.tile_pool(name="quantised", bufs=4))
         results = ctx.enter_context(tc.tile_pool(name="results", bufs=8))
-        flipped = ctx.enter_context(tc.psum_pool(name="flipped", bufs=4))
-        sums = ctx.enter_context(tc.psum_pool(name="sums", bufs=4))
+        flipped = ctx.enter_context(tc.psum_pool(name="flipped", bufs=3))
+        sums = ctx.enter_context(tc.psum_pool(name="sums", bufs=5))
         ctx.enter_context(tc.manual_schedule())
 
         zeros = keep.tile([P, 512], BF16, name="zeros")

@@ -19,6 +19,7 @@ HALVES = 2
 HALF = NODES // HALVES
 SLOTS = HALF // P
 F_CHUNKS = F_IN // P
+FLIP_BANKS = 3
 S_ROWS = 2 * P
 
 FLOPS = 2 * ((STEPS - 1) * NODES * NODES * F_IN + (2 * STEPS - 1) * NODES * F_IN * F_OUT)
@@ -35,7 +36,7 @@ def tile_stgnnlayer_pa_t_kernel(tc, X, S, w0, w1, out):
         grouped = ctx.enter_context(tc.tile_pool(name="grouped", bufs=2))
         quantised = ctx.enter_context(tc.tile_pool(name="quantised", bufs=4))
         results = ctx.enter_context(tc.tile_pool(name="results", bufs=8))
-        flipped = ctx.enter_context(tc.psum_pool(name="flipped", bufs=3))
+        flipped = ctx.enter_context(tc.psum_pool(name="flipped", bufs=FLIP_BANKS))
         sums = ctx.enter_context(tc.psum_pool(name="sums", bufs=5))
         ctx.enter_context(tc.manual_schedule())
 
@@ -118,7 +119,7 @@ def tile_stgnnlayer_pa_t_kernel(tc, X, S, w0, w1, out):
         w_mx = {}
 
         def flip_weights():
-            w0_ps = flipped.tile([P, 2, P], F32, name="w0_ps", tag="flipped")
+            w0_ps = sums.tile([P, 2, P], F32, name="w0_ps", tag="sums")
             for u in range(2):
                 nc.tensor.transpose(w0_ps[:, u, :], w_sb[0][:].bitcast(F32)[:, block(u)], ident_f32[:])
             w0_grouped = keep.tile([P, F_OUT * PACK], BF16, name="w0_grouped", align_bytes=64)
@@ -126,7 +127,7 @@ def tile_stgnnlayer_pa_t_kernel(tc, X, S, w0, w1, out):
                 out=w0_grouped[:].bitcast(F32).rearrange("p (o u) -> p o u", u=2),
                 in_=w0_ps[:].rearrange("p u o -> p o u"),
             )
-            w1_ps = flipped.tile([P, F_CHUNKS, P], BF16, name="w1_ps", tag="flipped")
+            w1_ps = sums.tile([P, F_CHUNKS, P], BF16, name="w1_ps", tag="sums")
             for c in range(F_CHUNKS):
                 nc.tensor.transpose(w1_ps[:, c, :], w_sb[1][:, block(c)], ident_bf16[:])
             w1_grouped = keep.tile([P, F_OUT * PACK], BF16, name="w1_grouped", align_bytes=64)
@@ -164,6 +165,9 @@ def tile_stgnnlayer_pa_t_kernel(tc, X, S, w0, w1, out):
         def quantise_xn(t, g):
             xn_mx[(t, g)] = quantise(xn_grouped[(t, g)][:], quantised, "xn")
 
+        waiting = []
+        unquantised = []
+
         def flip_x(t, h, b, engine):
             if b == 0:
                 if t == 0:
@@ -177,7 +181,13 @@ def tile_stgnnlayer_pa_t_kernel(tc, X, S, w0, w1, out):
             for i in range(2):
                 for u in range(2):
                     nc.tensor.transpose(xt_ps[:, i, u, :], words[:, 2 * b + i, block(u)], ident_f32[:])
-            copy_on(engine, pairs[:, 2 * b : 2 * b + 2, :, :], xt_ps[:].rearrange("p i u n -> p i n u"))
+            waiting.append((engine, pairs[:, 2 * b : 2 * b + 2, :, :], xt_ps[:].rearrange("p i u n -> p i n u"), (t, h, b)))
+
+        def empty_bank():
+            engine, to, source, which = waiting.pop(0)
+            copy_on(engine, to, source)
+            if which[2] == 1:
+                unquantised.append(which[:2])
 
         def quantise_xt(t, h):
             xt_mx[(t, h)] = quantise(xt_grouped[(t, h)][:], quantised, "xt")
@@ -235,7 +245,9 @@ def tile_stgnnlayer_pa_t_kernel(tc, X, S, w0, w1, out):
         warm(12)
         regroup_x(0, 0, 384)
         flip_x(0, 0, 0, True)
+        empty_bank()
         flip_x(0, 0, 1, True)
+        empty_bank()
         flip_s(0, True)
         warm(4)
         quantise_xn(0, 0)
@@ -260,14 +272,18 @@ def tile_stgnnlayer_pa_t_kernel(tc, X, S, w0, w1, out):
         shift(0, 0, 3)
         flip_s(6, False)
         flip_x(0, 1, 0, True)
+        empty_bank()
         flip_x(0, 1, 1, True)
+        empty_bank()
         regroup_x(1, 0)
         quantise_s(6)
         shift(0, 1, 0)
         shift(0, 1, 1)
         flip_s(7, True)
         flip_x(1, 0, 0, True)
+        empty_bank()
         flip_x(1, 0, 1, True)
+        empty_bank()
         regroup_x(1, 1)
         quantise_s(7)
         shift(0, 1, 2)
@@ -278,20 +294,21 @@ def tile_stgnnlayer_pa_t_kernel(tc, X, S, w0, w1, out):
         flip_weights()
         for b in range(2):
             flip_x(1, 1, b, True)
+            empty_bank()
+        unquantised.clear()
         quantise_xt(1, 0)
         quantise_weights()
         quantise_z(0, 1)
 
         banks = [(x, h, b) for x in range(2, STEPS) for h in range(HALVES) for b in range(2)]
-        done = []
         quantise_xt(1, 1)
         for n in range(SLOTS * HALVES, SLOTS * HALVES * (STEPS - 1)):
             t, slot = divmod(n, SLOTS * HALVES)
             h, j = divmod(slot, SLOTS)
             more = t + 1 < STEPS - 1
             shift(t, h, j)
-            if slot == 0 and more:
-                regroup_x(t + 1, 0)
+            if slot < 2 and more:
+                regroup_x(t + 1, slot)
             if slot == 3:
                 if more:
                     quantise_xn(t + 1, 0)
@@ -303,24 +320,22 @@ def tile_stgnnlayer_pa_t_kernel(tc, X, S, w0, w1, out):
                 quantise_z(t, 1)
             if n % 6 == 3 and banks:
                 for k in range(3):
-                    x, xh, b = banks.pop(0)
-                    flip_x(x, xh, b, True)
-                    if b == 1:
-                        done.append((x, xh))
-            if n % 6 == 5 and n > 12:
-                for x, xh in done:
-                    quantise_xt(x, xh)
-                done = []
-            if slot == 1 and more:
-                regroup_x(t + 1, 1)
+                    flip_x(*banks.pop(0), True)
+            if waiting:
+                empty_bank()
+            while waiting and not banks:
+                empty_bank()
+            if n % 6 == 0 or n == 53:
+                while unquantised:
+                    quantise_xt(*unquantised.pop(0))
             if t == STEPS - 2 and slot in (1, 2):
                 quantise_xt(0, slot - 1)
             if t == STEPS - 2 and slot in (4, 5):
                 taps(0, slot - 4)
         t = STEPS - 2
         quantise_z(t, 1, 0, 2)
-        taps(t, 1)
         quantise_z(t, 1, 2, 2)
+        taps(t, 1)
         taps(t + 1, 0, True)
         taps(t + 1, 1, True, 0, 2)
         taps(t + 1, 1, False, 2, 2)

@@ -88,8 +88,8 @@ def tile_stgnnlayer_pa_t_kernel(tc, X, S, w0, w1, out):
 
         def quantise(values, pool, label):
             width = values.shape[1] // PACK
-            codes = pool.tile([P, width], U32, name=label + "_codes", tag=label + "_codes", align_bytes=64)
-            scales = pool.tile([P, width], U8, name=label + "_scales", tag=label + "_scales", align_bytes=64)
+            codes = pool.tile([P, width], U32, name=label + "_codes", tag=label + "_codes", align_bytes=256)
+            scales = pool.tile([P, width], U8, name=label + "_scales", tag=label + "_scales", align_bytes=256)
             nc.vector.quantize_mx(out=codes[:].bitcast(FP8X4), scales=scales[:], in_=values)
             return codes, scales
 

@@ -313,10 +313,10 @@ def tile_stgnnlayer_pa_t_kernel(tc, X, S, w0, w1, out):
                 if more:
                     quantise_xn(t + 1, 0)
                     quantise_xn(t + 1, 1)
-                taps(t, 0)
+                taps(t, 0, t < 0)
                 quantise_z(t, 0)
             if slot == 7 and more:
-                taps(t, 1)
+                taps(t, 1, t < 0)
                 quantise_z(t, 1)
             if n % 6 == 3 and banks:
                 for k in range(3):
@@ -330,12 +330,13 @@ def tile_stgnnlayer_pa_t_kernel(tc, X, S, w0, w1, out):
                     quantise_xt(*unquantised.pop(0))
             if t == STEPS - 2 and slot in (1, 2):
                 quantise_xt(0, slot - 1)
+            if n == 51:
+                taps(t, 1)
             if t == STEPS - 2 and slot in (4, 5):
                 taps(0, slot - 4)
         t = STEPS - 2
         quantise_z(t, 1, 0, 2)
         quantise_z(t, 1, 2, 2)
-        taps(t, 1)
         taps(t + 1, 0, True)
         taps(t + 1, 1, True, 0, 2)
         taps(t + 1, 1, False, 2, 2)

@@ -82,9 +82,22 @@ def tile_stgnnlayer_pa_t_kernel(tc, X, S, w0, w1, out):
             load_s(s)
         for tap in range(2):
             load_w(tap)
-        for t in range(1, STEPS):
+        for t in range(1, STEPS - 1):
             for h in range(HALVES):
                 load_x(t, h)
+
+        last_sb = {}
+        pieces = [(h, q, u, e) for h in range(HALVES) for q in range(4) for u in range(2) for e in range(2)]
+
+        def load_last(h, q, u, e):
+            if (q, u, e) == (0, 0, 0):
+                last_half = keep.tile([P, SLOTS * F_IN], BF16, name="x_last_%d" % h, align_bytes=64)
+                last_sb[h] = last_half
+            nodes = X[0, STEPS - 1, h * HALF : (h + 1) * HALF, :].rearrange("(b m e) f -> m e b f", m=16, e=2)
+            nc.sync.dma_start(
+                out=last_sb[h][32 * q + u : 32 * (q + 1) : 2, :].rearrange("m (e b k) -> m e b k", e=2, b=16)[:, e, :, :],
+                in_=nodes[:, e, :, 256 * u + 64 * q : 256 * u + 64 * (q + 1)],
+            )
 
         def quantise(values, pool, label):
             width = values.shape[1] // PACK
@@ -189,6 +202,11 @@ def tile_stgnnlayer_pa_t_kernel(tc, X, S, w0, w1, out):
             if which[2] == 1:
                 unquantised.append(which[:2])
 
+        def turn_last(h):
+            turned = grouped.tile([P, HALF * PACK], BF16, name="xt_last", tag="xt_last", align_bytes=64)
+            nc.vector.transpose(out=turned[:].bitcast(F32), in_=last_sb[h][:].bitcast(F32))
+            xt_grouped[(STEPS - 1, h)] = turned
+
         def quantise_xt(t, h):
             xt_mx[(t, h)] = quantise(xt_grouped[(t, h)][:], quantised, "xt")
 
@@ -231,7 +249,9 @@ def tile_stgnnlayer_pa_t_kernel(tc, X, S, w0, w1, out):
         def taps(t, h, engine=False, first=0, slots=SLOTS):
             y_ps = sums.tile([P, slots, F_OUT], F32, name="y_ps", tag="sums")
             for j in range(slots):
-                mx_pass(y_ps[:, j, :], xt_mx[(t, h)], first + j, w_mx[0], 0, True, t == 0)
+                slot = first + j
+                i = slot if t < STEPS - 1 else 2 * (slot % 2) + slot // 2
+                mx_pass(y_ps[:, j, :], xt_mx[(t, h)], i, w_mx[0], 0, True, t == 0)
                 if t > 0:
                     operand, i = z_mx[(t - 1, h, first + j)]
                     mx_pass(y_ps[:, j, :], operand, i, w_mx[1], 0, False, True)
@@ -300,7 +320,7 @@ def tile_stgnnlayer_pa_t_kernel(tc, X, S, w0, w1, out):
         quantise_weights()
         quantise_z(0, 1)
 
-        banks = [(x, h, b) for x in range(2, STEPS) for h in range(HALVES) for b in range(2)]
+        banks = [(x, h, b) for x in range(2, STEPS - 1) for h in range(HALVES) for b in range(2)]
         quantise_xt(1, 1)
         for n in range(SLOTS * HALVES, SLOTS * HALVES * (STEPS - 1)):
             t, slot = divmod(n, SLOTS * HALVES)
@@ -313,27 +333,34 @@ def tile_stgnnlayer_pa_t_kernel(tc, X, S, w0, w1, out):
                 if more:
                     quantise_xn(t + 1, 0)
                     quantise_xn(t + 1, 1)
-                taps(t, 0, t < 0)
+                taps(t, 0, t > 0)
                 quantise_z(t, 0)
             if slot == 7 and more:
                 taps(t, 1, t < 0)
                 quantise_z(t, 1)
             if n % 6 == 3 and banks:
-                for k in range(3):
+                for k in range(min(3, len(banks))):
                     flip_x(*banks.pop(0), True)
             if waiting:
                 empty_bank()
             while waiting and not banks:
                 empty_bank()
-            if n % 6 == 0 or n == 53:
+            if n % 6 == 0 or n == 99:
                 while unquantised:
                     quantise_xt(*unquantised.pop(0))
-            if t == STEPS - 2 and slot in (1, 2):
-                quantise_xt(0, slot - 1)
+            for k in range(2):
+                if pieces and n >= 8:
+                    load_last(*pieces.pop(0))
+            if n in (36, 49):
+                turn_last(0 if n == 36 else 1)
+            if n in (38, 51):
+                quantise_xt(STEPS - 1, 0 if n == 38 else 1)
+            if n in (20, 21):
+                quantise_xt(0, 0 if n == 20 else 1)
             if n == 51:
                 taps(t, 1)
-            if t == STEPS - 2 and slot in (4, 5):
-                taps(0, slot - 4)
+            if n in (28, 29):
+                taps(0, 0 if n == 28 else 1)
         t = STEPS - 2
         quantise_z(t, 1, 0, 2)
         quantise_z(t, 1, 2, 2)

@@ -20,6 +20,7 @@ HALF = NODES // HALVES
 SLOTS = HALF // P
 F_CHUNKS = F_IN // P
 FLIP_BANKS = 3
+BY_VECTOR = (0, 7)
 S_ROWS = 2 * P
 
 FLOPS = 2 * ((STEPS - 1) * NODES * NODES * F_IN + (2 * STEPS - 1) * NODES * F_IN * F_OUT)
@@ -86,16 +87,18 @@ def tile_stgnnlayer_pa_t_kernel(tc, X, S, w0, w1, out):
             for h in range(HALVES):
                 load_x(t, h)
 
-        last_sb = {}
-        pieces = [(h, q, u, e) for h in range(HALVES) for q in range(4) for u in range(2) for e in range(2)]
+        blocks_sb = {}
+        pieces = [
+            (t, h, q, u, e) for t in BY_VECTOR for h in range(HALVES) for q in range(4) for u in range(2) for e in range(2)
+        ]
 
-        def load_last(h, q, u, e):
+        def load_piece(t, h, q, u, e):
             if (q, u, e) == (0, 0, 0):
-                last_half = keep.tile([P, SLOTS * F_IN], BF16, name="x_last_%d" % h, align_bytes=64)
-                last_sb[h] = last_half
-            nodes = X[0, STEPS - 1, h * HALF : (h + 1) * HALF, :].rearrange("(b m e) f -> m e b f", m=16, e=2)
+                blocks = keep.tile([P, SLOTS * F_IN], BF16, name="x_blocks_%d_%d" % (t, h), align_bytes=64)
+                blocks_sb[(t, h)] = blocks
+            nodes = X[0, t, h * HALF : (h + 1) * HALF, :].rearrange("(b m e) f -> m e b f", m=16, e=2)
             nc.sync.dma_start(
-                out=last_sb[h][32 * q + u : 32 * (q + 1) : 2, :].rearrange("m (e b k) -> m e b k", e=2, b=16)[:, e, :, :],
+                out=blocks_sb[(t, h)][32 * q + u : 32 * (q + 1) : 2, :].rearrange("m (e b k) -> m e b k", e=2, b=16)[:, e, :, :],
                 in_=nodes[:, e, :, 256 * u + 64 * q : 256 * u + 64 * (q + 1)],
             )
 
@@ -202,10 +205,10 @@ def tile_stgnnlayer_pa_t_kernel(tc, X, S, w0, w1, out):
             if which[2] == 1:
                 unquantised.append(which[:2])
 
-        def turn_last(h):
-            turned = grouped.tile([P, HALF * PACK], BF16, name="xt_last", tag="xt_last", align_bytes=64)
-            nc.vector.transpose(out=turned[:].bitcast(F32), in_=last_sb[h][:].bitcast(F32))
-            xt_grouped[(STEPS - 1, h)] = turned
+        def turn_x(t, h):
+            turned = grouped.tile([P, HALF * PACK], BF16, name="xt_turned", tag="xt_turned", align_bytes=64)
+            nc.vector.transpose(out=turned[:].bitcast(F32), in_=blocks_sb[(t, h)][:].bitcast(F32))
+            xt_grouped[(t, h)] = turned
 
         def quantise_xt(t, h):
             xt_mx[(t, h)] = quantise(xt_grouped[(t, h)][:], quantised, "xt")
@@ -250,7 +253,7 @@ def tile_stgnnlayer_pa_t_kernel(tc, X, S, w0, w1, out):
             y_ps = sums.tile([P, slots, F_OUT], F32, name="y_ps", tag="sums")
             for j in range(slots):
                 slot = first + j
-                i = slot if t < STEPS - 1 else 2 * (slot % 2) + slot // 2
+                i = slot if t not in BY_VECTOR else 2 * (slot % 2) + slot // 2
                 mx_pass(y_ps[:, j, :], xt_mx[(t, h)], i, w_mx[0], 0, True, t == 0)
                 if t > 0:
                     operand, i = z_mx[(t - 1, h, first + j)]
@@ -262,12 +265,8 @@ def tile_stgnnlayer_pa_t_kernel(tc, X, S, w0, w1, out):
                 in_=y_sb[:].rearrange("p (u r) -> p u r", r=2 * F_OUT),
             )
 
-        warm(12)
+        warm(14)
         regroup_x(0, 0, 384)
-        flip_x(0, 0, 0, True)
-        empty_bank()
-        flip_x(0, 0, 1, True)
-        empty_bank()
         flip_s(0, True)
         warm(4)
         quantise_xn(0, 0)
@@ -278,34 +277,30 @@ def tile_stgnnlayer_pa_t_kernel(tc, X, S, w0, w1, out):
         quantise_s(0)
         quantise_xn(0, 1)
         quantise_s(1)
-        flip_s(3, False)
+        flip_s(3, True)
         quantise_s(2)
         quantise_s(3)
 
         shift(0, 0, 0)
         shift(0, 0, 1)
         flip_s(4, False)
-        flip_s(5, False)
+        flip_s(5, True)
         quantise_s(4)
         quantise_s(5)
         shift(0, 0, 2)
         shift(0, 0, 3)
         flip_s(6, False)
-        flip_x(0, 1, 0, True)
-        empty_bank()
-        flip_x(0, 1, 1, True)
-        empty_bank()
+        flip_s(7, True)
         regroup_x(1, 0)
         quantise_s(6)
+        quantise_s(7)
         shift(0, 1, 0)
         shift(0, 1, 1)
-        flip_s(7, True)
         flip_x(1, 0, 0, True)
         empty_bank()
         flip_x(1, 0, 1, True)
         empty_bank()
         regroup_x(1, 1)
-        quantise_s(7)
         shift(0, 1, 2)
         shift(0, 1, 3)
         for g in range(2):
@@ -320,7 +315,8 @@ def tile_stgnnlayer_pa_t_kernel(tc, X, S, w0, w1, out):
         quantise_weights()
         quantise_z(0, 1)
 
-        banks = [(x, h, b) for x in range(2, STEPS - 1) for h in range(HALVES) for b in range(2)]
+        banks = [(x, h, b) for x in range(2, STEPS) if x not in BY_VECTOR for h in range(HALVES) for b in range(2)]
+        TURN = {21: (0, 0), 37: (0, 1), 45: (7, 0), 50: (7, 1)}
         quantise_xt(1, 1)
         for n in range(SLOTS * HALVES, SLOTS * HALVES * (STEPS - 1)):
             t, slot = divmod(n, SLOTS * HALVES)
@@ -348,19 +344,17 @@ def tile_stgnnlayer_pa_t_kernel(tc, X, S, w0, w1, out):
             if n % 6 == 0 or n == 99:
                 while unquantised:
                     quantise_xt(*unquantised.pop(0))
-            for k in range(2):
+            for k in range(3):
                 if pieces and n >= 8:
-                    load_last(*pieces.pop(0))
-            if n in (36, 49):
-                turn_last(0 if n == 36 else 1)
-            if n in (38, 51):
-                quantise_xt(STEPS - 1, 0 if n == 38 else 1)
-            if n in (20, 21):
-                quantise_xt(0, 0 if n == 20 else 1)
-            if n == 51:
+                    load_piece(*pieces.pop(0))
+            if n in TURN:
+                turn_x(*TURN[n])
+            if n - 3 in TURN:
+                quantise_xt(*TURN[n - 3])
+            if n == 52:
                 taps(t, 1)
-            if n in (28, 29):
-                taps(0, 0 if n == 28 else 1)
+            if n in (36, 44):
+                taps(0, 0 if n == 36 else 1)
         t = STEPS - 2
         quantise_z(t, 1, 0, 2)
         quantise_z(t, 1, 2, 2)

from contextlib import ExitStack

import concourse.mybir as mybir
from concourse.masks import make_identity

BF16 = mybir.dt.bfloat16
F32 = mybir.dt.float32
U32 = mybir.dt.uint32
U8 = mybir.dt.uint8
FP8X4 = mybir.dt.float8_e4m3fn_x4

P = 128
PACK = 4
STEPS = 8
NODES = 1024
F_IN = 512
F_OUT = 128
HALVES = 2
HALF = NODES // HALVES
SLOTS = HALF // P
F_CHUNKS = F_IN // P
FLIP_BANKS = 3
BY_VECTOR = (0, 7)
S_ROWS = 2 * P

FLOPS = 2 * ((STEPS - 1) * NODES * NODES * F_IN + (2 * STEPS - 1) * NODES * F_IN * F_OUT)


def block(i):
    return slice(i * P, (i + 1) * P)


def tile_stgnnlayer_pa_t_kernel(tc, X, S, w0, w1, out):
    nc = tc.nc
    with ExitStack() as ctx:
        keep = ctx.enter_context(tc.tile_pool(name="keep", bufs=1))
        grouped = ctx.enter_context(tc.tile_pool(name="grouped", bufs=2))
        quantised = ctx.enter_context(tc.tile_pool(name="quantised", bufs=4))
        results = ctx.enter_context(tc.tile_pool(name="results", bufs=8))
        flipped = ctx.enter_context(tc.psum_pool(name="flipped", bufs=FLIP_BANKS))
        sums = ctx.enter_context(tc.psum_pool(name="sums", bufs=5))
        ctx.enter_context(tc.manual_schedule())

        zeros = keep.tile([P, 512], BF16, name="zeros")
        nc.vector.memset(zeros[:], 0.0)
        ident_f32 = keep.tile([P, P], F32, name="ident_f32")
        make_identity(nc, ident_f32[:])
        ident_bf16 = keep.tile([P, P], BF16, name="ident_bf16")
        make_identity(nc, ident_bf16[:])

        x_sb = {}
        s_sb = {}
        w_sb = {}

        def load_x(t, h):
            x_half = keep.tile([P, SLOTS * F_IN], BF16, name="x_%d_%d" % (t, h))
            nc.sync.dma_start(
                out=x_half[:].rearrange("p (u r) -> p u r", u=2),
                in_=X[0, t, h * HALF : (h + 1) * HALF, :].rearrange("(u p e) f -> p u (e f)", u=2, e=2),
            )
            x_sb[(t, h)] = x_half

        def load_s(s):
            a, e = divmod(s, 2)
            s_slot = keep.tile([P, NODES], BF16, name="s_%d" % s)
            nc.sync.dma_start(
                out=s_slot[:],
                in_=S[a * S_ROWS : (a + 1) * S_ROWS, :].rearrange("(p e) m -> p e m", e=2)[:, e, :],
            )
            s_sb[s] = s_slot

        def load_w(tap):
            w_tap = keep.tile([P, F_IN], BF16, name="w%d_sb" % tap)
            nc.sync.dma_start(out=w_tap[:], in_=(w0, w1)[tap])
            w_sb[tap] = w_tap

        load_x(0, 0)
        load_s(0)
        load_x(0, 1)
        for s in range(1, SLOTS):
            load_s(s)
        for s in range(SLOTS, 2 * SLOTS):
            load_s(s)
        for tap in range(2):
            load_w(tap)
        for t in range(1, STEPS - 1):
            for h in range(HALVES):
                load_x(t, h)

        blocks_sb = {}
        pieces = [
            (t, h, q, u, e) for t in BY_VECTOR for h in range(HALVES) for q in range(4) for u in range(2) for e in range(2)
        ]

        def load_piece(t, h, q, u, e):
            if (q, u, e) == (0, 0, 0):
                blocks = keep.tile([P, SLOTS * F_IN], BF16, name="x_blocks_%d_%d" % (t, h), align_bytes=64)
                blocks_sb[(t, h)] = blocks
            nodes = X[0, t, h * HALF : (h + 1) * HALF, :].rearrange("(b m e) f -> m e b f", m=16, e=2)
            nc.sync.dma_start(
                out=blocks_sb[(t, h)][32 * q + u : 32 * (q + 1) : 2, :].rearrange("m (e b k) -> m e b k", e=2, b=16)[:, e, :, :],
                in_=nodes[:, e, :, 256 * u + 64 * q : 256 * u + 64 * (q + 1)],
            )

        def quantise(values, pool, label):
            width = values.shape[1] // PACK
            codes = pool.tile([P, width], U32, name=label + "_codes", tag=label + "_codes", align_bytes=256)
            scales = pool.tile([P, width], U8, name=label + "_scales", tag=label + "_scales", align_bytes=256)
            nc.vector.quantize_mx(out=codes[:].bitcast(FP8X4), scales=scales[:], in_=values)
            return codes, scales

        def mx_pass(acc, stationary, i, moving, k, start, stop):
            nc.tensor.matmul_mx(
                out=acc,
                lhsT=stationary[0][:, block(i)].bitcast(FP8X4),
                lhsT_scale=stationary[1][:, block(i)],
                rhs=moving[0][:, block(k)].bitcast(FP8X4),
                rhs_scale=moving[1][:, block(k)],
                start=start,
                stop=stop,
            )

        def copy_on(engine, out, in_):
            if engine:
                nc.scalar.copy(out=out, in_=in_)
            else:
                nc.vector.tensor_copy(out=out, in_=in_)

        def warm(n):
            warm_ps = sums.tile([P, 512], F32, name="warm_ps", tag="sums")
            for k in range(n):
                nc.tensor.matmul(warm_ps[:], lhsT=zeros[:, :P], rhs=zeros[:], start=True, stop=True)

        w_grouped = {}
        w_mx = {}

        def flip_weights():
            w0_ps = sums.tile([P, 2, P], F32, name="w0_ps", tag="sums")
            for u in range(2):
                nc.tensor.transpose(w0_ps[:, u, :], w_sb[0][:].bitcast(F32)[:, block(u)], ident_f32[:])
            w0_grouped = keep.tile([P, F_OUT * PACK], BF16, name="w0_grouped", align_bytes=64)
            nc.scalar.copy(
                out=w0_grouped[:].bitcast(F32).rearrange("p (o u) -> p o u", u=2),
                in_=w0_ps[:].rearrange("p u o -> p o u"),
            )
            w1_ps = sums.tile([P, F_CHUNKS, P], BF16, name="w1_ps", tag="sums")
            for c in range(F_CHUNKS):
                nc.tensor.transpose(w1_ps[:, c, :], w_sb[1][:, block(c)], ident_bf16[:])
            w1_grouped = keep.tile([P, F_OUT * PACK], BF16, name="w1_grouped", align_bytes=64)
            nc.scalar.copy(
                out=w1_grouped[:].rearrange("p (o c) -> p o c", c=F_CHUNKS),
                in_=w1_ps[:].rearrange("p c o -> p o c"),
            )
            w_grouped[0] = w0_grouped
            w_grouped[1] = w1_grouped

        def quantise_weights():
            for tap in range(2):
                w_mx[tap] = quantise(w_grouped[tap][:], keep, "w%d" % tap)

        xn_grouped = {}
        xn_mx = {}
        xt_grouped = {}
        xt_mx = {}
        st_grouped = {}
        st_mx = {}
        z_grouped = {}
        z_mx = {}

        def regroup_x(t, g, scalar_from=F_IN):
            values = grouped.tile([P, F_IN * PACK], BF16, name="xn_grouped", tag="xn_grouped", align_bytes=64)
            for lo, hi, engine in ((0, scalar_from, False), (scalar_from, F_IN, True)):
                if lo < hi:
                    copy_on(
                        engine,
                        values[:, lo * PACK : hi * PACK].rearrange("p (c i j) -> p c j i", i=4, j=PACK),
                        x_sb[(t, g)][:].rearrange("p (j f) -> p j f", j=PACK)[:, :, lo:hi].rearrange("p j (c i) -> p c j i", i=4),
                    )
            xn_grouped[(t, g)] = values

        def quantise_xn(t, g):
            xn_mx[(t, g)] = quantise(xn_grouped[(t, g)][:], quantised, "xn")

        waiting = []
        unquantised = []

        def flip_x(t, h, b, engine):
            if b == 0:
                if t == 0:
                    values = keep.tile([P, HALF * PACK], BF16, name="xt_grouped_0_%d" % h, align_bytes=64)
                else:
                    values = grouped.tile([P, HALF * PACK], BF16, name="xt_grouped", tag="xt_grouped", bufs=3, align_bytes=64)
                xt_grouped[(t, h)] = values
            pairs = xt_grouped[(t, h)][:].bitcast(F32).rearrange("p (j n u) -> p j n u", j=SLOTS, u=2)
            words = x_sb[(t, h)][:].bitcast(F32).rearrange("p (j w) -> p j w", j=SLOTS)
            xt_ps = flipped.tile([P, 2, 2, P], F32, name="xt_ps", tag="flipped")
            for i in range(2):
                for u in range(2):
                    nc.tensor.transpose(xt_ps[:, i, u, :], words[:, 2 * b + i, block(u)], ident_f32[:])
            waiting.append((engine, pairs[:, 2 * b : 2 * b + 2, :, :], xt_ps[:].rearrange("p i u n -> p i n u"), (t, h, b)))

        def empty_bank():
            engine, to, source, which = waiting.pop(0)
            copy_on(engine, to, source)
            if which[2] == 1:
                unquantised.append(which[:2])

        def turn_x(t, h):
            turned = grouped.tile([P, HALF * PACK], BF16, name="xt_turned", tag="xt_turned", align_bytes=64)
            nc.vector.transpose(out=turned[:].bitcast(F32), in_=blocks_sb[(t, h)][:].bitcast(F32))
            xt_grouped[(t, h)] = turned

        def quantise_xt(t, h):
            xt_mx[(t, h)] = quantise(xt_grouped[(t, h)][:], quantised, "xt")

        def flip_s(s, engine):
            values = grouped.tile([P, HALVES * P * PACK], BF16, name="st_grouped", tag="st_grouped", bufs=4, align_bytes=64)
            words = s_sb[s][:].bitcast(F32)
            st_ps = sums.tile([P, 2 * HALVES, P], F32, name="st_ps", tag="sums")
            for k in range(2 * HALVES):
                nc.tensor.transpose(st_ps[:, k, :], words[:, block(k)], ident_f32[:])
            copy_on(
                engine,
                values[:].bitcast(F32).rearrange("p (g n u) -> p g n u", g=HALVES, u=2),
                st_ps[:].rearrange("p (g u) n -> p g n u", u=2),
            )
            st_grouped[s] = values

        def quantise_s(s):
            st_mx[s] = quantise(st_grouped[s][:], keep, "st_%d" % s)

        def shift(t, h, j, engine=True):
            if j == 0:
                z_half = grouped.tile([P, HALF * PACK], BF16, name="z_grouped", tag="z_grouped", align_bytes=64)
                z_grouped[(t, h)] = z_half
            z_ps = sums.tile([P, F_CHUNKS, P], F32, name="z_ps", tag="sums")
            for c in range(F_CHUNKS):
                for g in range(HALVES):
                    mx_pass(z_ps[:, c, :], xn_mx[(t, g)], c, st_mx[SLOTS * h + j], g, g == 0, g == HALVES - 1)
            copy_on(
                engine,
                z_grouped[(t, h)][:].rearrange("p (j n c) -> p j n c", j=SLOTS, c=F_CHUNKS)[:, j, :, :],
                z_ps[:].rearrange("p c n -> p n c"),
            )

        def quantise_z(t, h, first=0, slots=SLOTS):
            values = z_grouped[(t, h)][:, first * P * PACK : (first + slots) * P * PACK]
            operand = quantise(values, quantised, "z" if slots == SLOTS else "z_part")
            for j in range(slots):
                z_mx[(t, h, first + j)] = (operand, j)

        def taps(t, h, engine=False, first=0, slots=SLOTS):
            y_ps = sums.tile([P, slots, F_OUT], F32, name="y_ps", tag="sums")
            for j in range(slots):
                slot = first + j
                i = slot if t not in BY_VECTOR else 2 * (slot % 2) + slot // 2
                mx_pass(y_ps[:, j, :], xt_mx[(t, h)], i, w_mx[0], 0, True, t == 0)
                if t > 0:
                    operand, i = z_mx[(t - 1, h, first + j)]
                    mx_pass(y_ps[:, j, :], operand, i, w_mx[1], 0, False, True)
            y_sb = results.tile([P, slots * F_OUT], F32, name="y_sb", tag="y_sb")
            copy_on(engine, y_sb[:], y_ps[:].rearrange("p j o -> p (j o)"))
            nc.sync.dma_start(
                out=out[0, t, h * HALF : (h + 1) * HALF, :].rearrange("(u p e) o -> p u (e o)", u=2, e=2)[:, first // 2 : (first + slots) // 2, :],
                in_=y_sb[:].rearrange("p (u r) -> p u r", r=2 * F_OUT),
            )

        warm(14)
        regroup_x(0, 0, 384)
        flip_s(0, True)
        warm(4)
        quantise_xn(0, 0)
        regroup_x(0, 1, 384)
        flip_s(1, True)
        flip_s(2, True)
        warm(1)
        quantise_s(0)
        quantise_xn(0, 1)
        quantise_s(1)
        flip_s(3, True)
        quantise_s(2)
        quantise_s(3)

        shift(0, 0, 0)
        shift(0, 0, 1)
        flip_s(4, False)
        flip_s(5, True)
        quantise_s(4)
        quantise_s(5)
        shift(0, 0, 2)
        shift(0, 0, 3)
        flip_s(6, False)
        flip_s(7, True)
        regroup_x(1, 0)
        quantise_s(6)
        quantise_s(7)
        shift(0, 1, 0)
        shift(0, 1, 1)
        flip_x(1, 0, 0, True)
        empty_bank()
        flip_x(1, 0, 1, True)
        empty_bank()
        regroup_x(1, 1)
        shift(0, 1, 2)
        shift(0, 1, 3)
        for g in range(2):
            quantise_xn(1, g)
        quantise_z(0, 0)
        flip_weights()
        for b in range(2):
            flip_x(1, 1, b, True)
            empty_bank()
        unquantised.clear()
        quantise_xt(1, 0)
        quantise_weights()
        quantise_z(0, 1)

        banks = [(x, h, b) for x in range(2, STEPS) if x not in BY_VECTOR for h in range(HALVES) for b in range(2)]
        TURN = {21: (0, 0), 37: (0, 1), 45: (7, 0), 50: (7, 1)}
        quantise_xt(1, 1)
        for n in range(SLOTS * HALVES, SLOTS * HALVES * (STEPS - 1)):
            t, slot = divmod(n, SLOTS * HALVES)
            h, j = divmod(slot, SLOTS)
            more = t + 1 < STEPS - 1
            shift(t, h, j)
            if slot < 2 and more:
                regroup_x(t + 1, slot)
            if slot == 3:
                if more:
                    quantise_xn(t + 1, 0)
                    quantise_xn(t + 1, 1)
                taps(t, 0, t > 0)
                quantise_z(t, 0)
            if slot == 7 and more:
                taps(t, 1, t < 0)
                quantise_z(t, 1)
            if n % 6 == 3 and banks:
                for k in range(min(3, len(banks))):
                    flip_x(*banks.pop(0), True)
            if waiting:
                empty_bank()
            while waiting and not banks:
                empty_bank()
            if n % 6 == 0 or n == 99:
                while unquantised:
                    quantise_xt(*unquantised.pop(0))
            for k in range(3):
                if pieces and n >= 8:
                    load_piece(*pieces.pop(0))
            if n in TURN:
                turn_x(*TURN[n])
            if n - 3 in TURN:
                quantise_xt(*TURN[n - 3])
            if n == 52:
                taps(t, 1)
            if n in (36, 44):
                taps(0, 0 if n == 36 else 1)
        t = STEPS - 2
        quantise_z(t, 1, 0, 2)
        quantise_z(t, 1, 2, 2)
        taps(t + 1, 0, True)
        taps(t + 1, 1, True, 0, 2)
        taps(t + 1, 1, False, 2, 2)
